import numpy as np
import ml_dtypes


def mxq(x, axis, fmt="e4m3"):
    dtype, down = {"e4m3": (ml_dtypes.float8_e4m3fn, 7), "e5m2": (ml_dtypes.float8_e5m2, 14)}[fmt]
    v = np.moveaxis(np.asarray(x, np.float32).astype(ml_dtypes.bfloat16).astype(np.float64), axis, -1)
    blocks = v.reshape(v.shape[:-1] + (-1, 32))
    amax = np.abs(blocks).max(-1, keepdims=True)
    byte = np.maximum(np.where(amax > 0, np.frexp(amax)[1] - 1 + 127, 0) - down, 1)
    scale = np.exp2(byte - 127.0)
    codes = (blocks / scale).astype(np.float32).astype(dtype).astype(np.float64)
    return np.moveaxis((codes * scale).reshape(v.shape), -1, axis)


WIDE = False


def mx_kscale(k):
    if not WIDE:
        return np.ones(k)
    levels = np.array([10, -10, 5, -5, 0])
    if k % 512:
        return np.exp2(np.random.permutation(np.resize(levels, k // 32))).repeat(32)
    a = np.empty((k // 512, 16))
    for p in range(k // 512):
        a[p, :8] = np.random.permutation(np.resize(levels, 8))
        for g in range(8):
            far = levels[np.abs(levels - a[p, g]) >= 10]
            a[p, g + 8] = far[np.random.randint(len(far))]
    return np.exp2(a.ravel()).repeat(32)


BF16 = ml_dtypes.bfloat16


def bf(x):
    return np.asarray(x, np.float32).astype(BF16)


def f64(x):
    return np.asarray(x).astype(np.float64)


B, L, D, F = 128, 8, 512, 1024
EPS = 1e-12


def l2norm(w, axis):
    n = np.sqrt(np.sum(w * w, axis=axis, keepdims=True))
    return w / np.maximum(n, EPS)


def silu(z):
    return z / (1.0 + np.exp(-z))


def draw_w(k, n, s):
    a = np.random.standard_normal((L, k, n)) / s[:, None]
    return a / np.sqrt(np.sum(a * a, axis=1, keepdims=True)) * np.exp2(np.random.randint(-1, 2, (L, 1, n)))


def draw_gain():
    return np.random.choice([-1.0, 1.0], (1, F)) * (1.0 + 0.1 * np.random.standard_normal((1, F)))


def setup_inputs():
    s, t = mx_kscale(D), mx_kscale(F)
    c = np.sqrt(np.mean(1.0 / s**2))
    return {'x': bf(np.random.standard_normal((B, L, D)) * s),
            'W_gate': bf(draw_w(D, F, s)),
            'W_up': bf(draw_w(D, F, s)),
            'W_down': bf(draw_w(F, D, t)),
            's_u': bf(draw_gain() * c * t),
            's_v': bf(draw_gain() * c * 1.5 / np.sqrt(D))}


def reference(x, W_gate, W_up, W_down, s_u, s_v):
    Wg = l2norm(f64(W_gate), 1)
    Wu = l2norm(f64(W_up), 1)
    Wd = l2norm(f64(W_down), 1)
    xq = mxq(f64(x), 2, 'e4m3').transpose(1, 0, 2)
    u = f64(bf(xq @ mxq(Wg, 1, 'e4m3')))
    v = f64(bf(xq @ mxq(Wu, 1, 'e4m3')))
    u_scale = np.abs(f64(s_u)) * 1.0
    v_scale = np.abs(f64(s_v)) * np.sqrt(D)
    h = silu(v_scale * v) * (u_scale * u)
    out = (mxq(h, 2, 'e4m3') @ mxq(Wd, 1, 'e4m3')).transpose(1, 0, 2)
    return l2norm(out, -1)

@@ -1,0 +1,273 @@
+from contextlib import ExitStack
+import math
+
+import concourse.mybir as mybir
+from concourse.masks import make_identity
+
+B, L, D, F = 128, 8, 512, 1024
+FLOPS = 2 * B * L * (2 * D * F + F * D)
+
+F32 = mybir.dt.float32
+BF16 = mybir.dt.bfloat16
+U32 = mybir.dt.uint32
+U8 = mybir.dt.uint8
+FP8X4 = mybir.dt.float8_e4m3fn_x4
+ACT = mybir.ActivationFunctionType
+ALU = mybir.AluOpType
+
+P = 128
+EPS_SQ = 1e-24
+UV_DT = BF16
+LEAD = 2
+
+
+def tile_npertokenswishglu_kernel(tc, x, W_gate, W_up, W_down, s_u, s_v, out):
+    nc = tc.nc
+    with ExitStack() as ctx:
+        const = ctx.enter_context(tc.tile_pool(name="const", bufs=1))
+        rawp = ctx.enter_context(tc.tile_pool(name="rawp", bufs=6))
+        grpp = ctx.enter_context(tc.tile_pool(name="grpp", bufs=3))
+        codep = ctx.enter_context(tc.tile_pool(name="codep", bufs=5))
+        small = ctx.enter_context(tc.tile_pool(name="small", bufs=6))
+        junkp = ctx.enter_context(tc.tile_pool(name="junkp", bufs=2))
+        ep = ctx.enter_context(tc.tile_pool(name="ep", bufs=2))
+        psum = ctx.enter_context(tc.psum_pool(name="psum", bufs=1))
+
+        ident = const.tile([P, P], F32, name="ident")
+        make_identity(nc, ident[:])
+        mhalf = const.tile([P, 8], F32, name="mhalf")
+        nc.gpsimd.memset(mhalf[:], -0.5)
+        warm = const.tile([P, 1], F32, name="warm")
+        nc.scalar.activation(out=warm[:], in_=mhalf[:, 0:1], func=ACT.Silu)
+
+        su_raw = const.tile([P, 8], BF16, name="su_raw")
+        sv_raw = const.tile([P, 8], BF16, name="sv_raw")
+        nc.scalar.dma_start(out=su_raw[:].rearrange("p (g t) -> p g t", g=2), in_=s_u.rearrange("o (g p t) -> p (o g) t", g=2, t=4))
+        nc.scalar.dma_start(out=sv_raw[:].rearrange("p (g t) -> p g t", g=2), in_=s_v.rearrange("o (g p t) -> p (o g) t", g=2, t=4))
+
+        raws = {}
+
+        def load_unit(i):
+            l, mat = divmod(i, 3)
+            raw = rawp.tile([P, 4096], BF16, name="raw", tag="raw")
+            if i == 0:
+                for b in range(4):
+                    nc.sync.dma_start(
+                        out=raw[:].rearrange("p (j c) -> p j c", j=4)[:, :, 256 * b : 256 * (b + 1)],
+                        in_=W_gate[l].rearrange("(p j) c -> p j c", j=4)[:, :, 256 * b : 256 * (b + 1)],
+                    )
+            elif mat < 2:
+                w = W_gate if mat == 0 else W_up
+                nc.sync.dma_start(
+                    out=raw[:].rearrange("p (j c) -> p j c", j=4),
+                    in_=w[l].rearrange("(p j) c -> p j c", j=4),
+                )
+            else:
+                nc.sync.dma_start(
+                    out=raw[:].rearrange("p (h j c) -> p h j c", h=2, j=4),
+                    in_=W_down[l].rearrange("(h p j) c -> p h j c", h=2, j=4),
+                )
+            raws[i] = raw
+
+        load_unit(0)
+
+        x_sb = const.tile([P, L * D], BF16, name="x_sb")
+        nc.sync.dma_start(out=x_sb[:].rearrange("p (l d) -> p l d", l=L), in_=x)
+        load_unit(1)
+        load_unit(2)
+        load_unit(3)
+
+        def rsqrt_cols(dst, src):
+            n = src.shape[1]
+            clamped = small.tile([P, 8], F32, name="clamped", tag="clamped")
+            nc.gpsimd.tensor_scalar(out=clamped[:, 0:n], in0=src, scalar1=EPS_SQ, scalar2=None, op0=ALU.max)
+            nc.gpsimd.tensor_tensor(out=dst, in0=clamped[:, 0:n], in1=mhalf[:, 0:n], op=ALU.pow)
+
+        def norms(i):
+            mat = i % 3
+            words = raws[i][:].bitcast(F32)
+            nsq = small.tile([P, 8], F32, name="nsq", tag="nsq")
+            rn = small.tile([P, 8], F32, name="rn", tag="rn")
+            for bank in range(4):
+                wt = psum.tile([P, 4, P], F32, name="wt", tag="wt", bufs=3)
+                hi, lo = divmod(bank, 2)
+                for j in range(4):
+                    if mat < 2:
+                        off = 512 * j + 128 * bank
+                    else:
+                        off = 1024 * lo + 256 * j + 128 * hi
+                    nc.tensor.transpose(wt[:, j, :], words[:, off : off + 128], ident[:])
+                halves = wt[:].rearrange("p j q -> p (j q)").bitcast(BF16).rearrange("p (n e) -> p e n", e=2)
+                for e in range(2):
+                    if mat < 2:
+                        col = 4 * hi + 2 * e + lo
+                    else:
+                        col = 4 * lo + 2 * e + hi
+                    junk = junkp.tile([P, 512], BF16, name="junk", tag="junk")
+                    nc.scalar.activation(out=junk[:], in_=halves[:, e, :], func=ACT.Square, accum_out=nsq[:, col : col + 1])
+                if mat < 2 and lo == 1:
+                    rsqrt_cols(rn[:, 4 * hi : 4 * hi + 4], nsq[:, 4 * hi : 4 * hi + 4])
+            if mat == 2:
+                tot = small.tile([P, 4], F32, name="tot", tag="tot")
+                nc.gpsimd.tensor_tensor(out=tot[:], in0=nsq[:, 0:4], in1=nsq[:, 4:8], op=ALU.add)
+                rsqrt_cols(rn[:, 0:4], tot[:])
+            return rn
+
+        def spread(rn, c0):
+            rnb = psum.tile([P, 512], F32, name="rnb", tag="rnb", bufs=2)
+            for k in range(4):
+                nc.tensor.transpose(rnb[:, 128 * k : 128 * (k + 1)], rn[:, c0 + k : c0 + k + 1].to_broadcast([P, P]), ident[:])
+            return rnb
+
+        rns = {}
+        grps = {}
+        codes = {}
+        scales = {}
+        rnbs = {}
+
+        def prefetch(i):
+            if 4 <= i + 4 < 3 * L:
+                load_unit(i + 4)
+            if LEAD <= i + LEAD < 3 * L:
+                rns[i + LEAD] = norms(i + LEAD)
+
+        def scale(i, half):
+            mat = i % 3
+            if half == 0:
+                grps[i] = grpp.tile([P, 4096], BF16, name="grp", tag="grp", align_bytes=64)
+                codes[i] = codep.tile([P, 1024], U32, name="wcodes", tag="wcodes", align_bytes=64)
+                scales[i] = codep.tile([P, 1024], U8, name="wscales", tag="wscales", align_bytes=64)
+            chunk = raws[i][:, 2048 * half : 2048 * (half + 1)] if mat == 2 else None
+            dst = grps[i][:, 2048 * half : 2048 * (half + 1)]
+            if mat < 2:
+                rnb = spread(rns[i], 4 * half)
+                rv = raws[i][:].rearrange("p (j c) -> p j c", j=4)[:, :, 512 * half : 512 * (half + 1)]
+                rv = rv.rearrange("p j (m a e) -> p m a e j", a=2, e=2)
+                gv = dst.rearrange("p (a e m j) -> p m a e j", a=2, e=2, j=4)
+                bv = rnb[:].rearrange("p (e m a) -> p m a e", e=2, a=2).unsqueeze(4).to_broadcast([P, P, 2, 2, 4])
+            else:
+                if half == 0:
+                    rnbs[i] = spread(rns[i], 0)
+                rnb = rnbs[i]
+                rv = chunk.rearrange("p (j c e) -> p c e j", j=4, e=2)
+                gv = dst.rearrange("p (c e j) -> p c e j", e=2, j=4)
+                bv = rnb[:].rearrange("p (e c) -> p c e", e=2).unsqueeze(3).to_broadcast([P, 256, 2, 4])
+            nc.vector.tensor_tensor(out=gv, in0=rv, in1=bv, op=ALU.mult)
+
+        def quantise(i, lo, hi):
+            nc.vector.quantize_mx(
+                out=codes[i][:, lo // 4 : hi // 4].bitcast(FP8X4), scales=scales[i][:, lo // 4 : hi // 4], in_=grps[i][:, lo:hi]
+            )
+
+        uv = {}
+        hgs = {}
+
+        def stage1(l, g):
+            u_ps = psum.tile([P, 4, P], UV_DT, name="u_ps", tag="uv", bufs=2)
+            v_ps = psum.tile([P, 4, P], UV_DT, name="v_ps", tag="uv", bufs=2)
+            for dst, i in ((v_ps, 3 * l + 1), (u_ps, 3 * l)):
+                for t in range(4):
+                    cols = slice(512 * g + 128 * t, 512 * g + 128 * (t + 1))
+                    nc.tensor.matmul_mx(
+                        out=dst[:, t, :],
+                        lhsT=codes[i][:, cols].bitcast(FP8X4),
+                        lhsT_scale=scales[i][:, cols],
+                        rhs=x_codes[:, 128 * l : 128 * (l + 1)].bitcast(FP8X4),
+                        rhs_scale=x_scales[:, 128 * l : 128 * (l + 1)],
+                        start=True,
+                        stop=True,
+                    )
+            s1 = ep.tile([P, 4, P], F32, name="s1", tag="s1")
+            for t in range(4):
+                nc.scalar.activation(out=s1[:, t, :], in_=v_ps[:, t, :], func=ACT.Silu, scale=vs[:, 4 * g + t : 4 * g + t + 1])
+            uv[(l, g)] = (u_ps, s1)
+
+        def hidden(l, g):
+            u_ps, s1 = uv[(l, g)]
+            h_t = ep.tile([P, 4, P], BF16, name="h_t", tag="h_t")
+            for t in range(4):
+                nc.vector.scalar_tensor_tensor(
+                    out=h_t[:, t, :], in0=u_ps[:, t, :], scalar=us[:, 4 * g + t : 4 * g + t + 1], in1=s1[:, t, :],
+                    op0=ALU.mult, op1=ALU.mult,
+                )
+            nc.scalar.copy(
+                out=hgs[l][:, 512 * g : 512 * (g + 1)].rearrange("p (n t) -> p n t", t=4),
+                in_=h_t[:].rearrange("p t n -> p n t"),
+            )
+
+        def down(l):
+            i = 3 * l + 2
+            h_codes = ep.tile([P, 256], U32, name="h_codes", tag="h_codes", align_bytes=64)
+            h_scales = ep.tile([P, 256], U8, name="h_scales", tag="h_scales", align_bytes=64)
+            nc.vector.quantize_mx(out=h_codes[:].bitcast(FP8X4), scales=h_scales[:], in_=hgs[l][:])
+            o_ps = psum.tile([P, 512], F32, name="o_ps", tag="o", bufs=1)
+            for g in range(2):
+                nc.tensor.matmul_mx(
+                    out=o_ps[:],
+                    lhsT=h_codes[:, 128 * g : 128 * (g + 1)].bitcast(FP8X4),
+                    lhsT_scale=h_scales[:, 128 * g : 128 * (g + 1)],
+                    rhs=codes[i][:, 512 * g : 512 * (g + 1)].bitcast(FP8X4),
+                    rhs_scale=scales[i][:, 512 * g : 512 * (g + 1)],
+                    start=(g == 0),
+                    stop=(g == 1),
+                )
+            ss = small.tile([P, 1], F32, name="ss", tag="ss")
+            junk = junkp.tile([P, 512], BF16, name="junk", tag="junk")
+            nc.scalar.activation(out=junk[:], in_=o_ps[:], func=ACT.Square, accum_out=ss[:])
+            rno = small.tile([P, 1], F32, name="rno", tag="rno")
+            rsqrt_cols(rno[:], ss[:])
+            o_sb = ep.tile([P, 512], F32, name="o_sb", tag="o_sb")
+            nc.scalar.activation(out=o_sb[:], in_=o_ps[:], func=ACT.Copy, scale=rno[:, 0:1])
+            nc.sync.dma_start(out=out[:, l, :], in_=o_sb[:])
+
+        rns[0] = norms(0)
+
+        xw = x_sb[:].bitcast(F32)
+        xg = const.tile([P, L * D], BF16, name="xg", align_bytes=64)
+        xgw = xg[:].bitcast(F32)
+        for lp in range(L // 2):
+            xt = psum.tile([P, 4, P], F32, name="xt", tag="wt", bufs=3)
+            for l2 in range(2):
+                for u in range(2):
+                    l = 2 * lp + l2
+                    nc.tensor.transpose(xt[:, 2 * l2 + u, :], xw[:, 256 * l + u : 256 * (l + 1) : 2], ident[:])
+            nc.scalar.copy(
+                out=xgw[:, 512 * lp : 512 * (lp + 1)].rearrange("p (a n u) -> p a n u", a=2, u=2),
+                in_=xt[:].rearrange("p (a u) n -> p a n u", a=2),
+            )
+        us = const.tile([P, 8], F32, name="us")
+        vs = const.tile([P, 8], F32, name="vs")
+        nc.scalar.activation(out=us[:], in_=su_raw[:], func=ACT.Abs)
+        nc.scalar.activation(out=vs[:], in_=sv_raw[:], func=ACT.Abs, scale=math.sqrt(D))
+        x_codes = const.tile([P, L * P], U32, name="x_codes", align_bytes=64)
+        x_scales = const.tile([P, L * P], U8, name="x_scales", align_bytes=64)
+
+        for i in range(1, LEAD):
+            rns[i] = norms(i)
+
+        with tc.manual_schedule(engines={mybir.EngineType.DVE}):
+            for l in range(L):
+                ig, iu, idn = 3 * l, 3 * l + 1, 3 * l + 2
+                hgs[l] = ep.tile([P, 1024], BF16, name="hg", tag="hg", align_bytes=64)
+                prefetch(ig)
+                scale(ig, 0)
+                if l > 0:
+                    down(l - 1)
+                scale(ig, 1)
+                prefetch(iu)
+                scale(iu, 0)
+                quantise(ig, 0, 4096)
+                if l == 0:
+                    nc.vector.quantize_mx(out=x_codes[:].bitcast(FP8X4), scales=x_scales[:], in_=xg[:])
+                scale(iu, 1)
+                quantise(iu, 0, 2048)
+                stage1(l, 0)
+                quantise(iu, 2048, 4096)
+                prefetch(idn)
+                scale(idn, 0)
+                hidden(l, 0)
+                stage1(l, 1)
+                scale(idn, 1)
+                hidden(l, 1)
+                quantise(idn, 0, 4096)
+            down(L - 1)

@@ -40,10 +40,15 @@ def tile_npertokenswishglu_kernel(tc, x, W_gate, W_up, W_down, s_u, s_v, out):
         warm = const.tile([P, 1], F32, name="warm")
         nc.scalar.activation(out=warm[:], in_=mhalf[:, 0:1], func=ACT.Silu)
 
-        su_raw = const.tile([P, 8], BF16, name="su_raw")
-        sv_raw = const.tile([P, 8], BF16, name="sv_raw")
-        nc.scalar.dma_start(out=su_raw[:].rearrange("p (g t) -> p g t", g=2), in_=s_u.rearrange("o (g p t) -> p (o g) t", g=2, t=4))
-        nc.scalar.dma_start(out=sv_raw[:].rearrange("p (g t) -> p g t", g=2), in_=s_v.rearrange("o (g p t) -> p (o g) t", g=2, t=4))
+        gains_raw = const.tile([P, 32], BF16, name="gains_raw")
+
+        def load_gains():
+            for w, src_v in enumerate((s_v, s_u)):
+                for b in range(2):
+                    nc.sync.dma_start(
+                        out=gains_raw[b:P:2, 16 * w : 16 * (w + 1)].rearrange("p (g k) -> p g k", g=2),
+                        in_=src_v.rearrange("o (g s k) -> s (o g) k", g=2, k=8),
+                    )
 
         raws = {}
 
@@ -63,10 +68,12 @@ def tile_npertokenswishglu_kernel(tc, x, W_gate, W_up, W_down, s_u, s_v, out):
                     in_=w[l].rearrange("(p j) c -> p j c", j=4),
                 )
             else:
-                nc.sync.dma_start(
-                    out=raw[:].rearrange("p (h j c) -> p h j c", h=2, j=4),
-                    in_=W_down[l].rearrange("(h p j) c -> p h j c", h=2, j=4),
-                )
+                for h in range(2):
+                    for b in range(2):
+                        nc.sync.dma_start(
+                            out=raw[b:P:2, 2048 * h : 2048 * (h + 1)].rearrange("p (j c) -> p j c", j=4),
+                            in_=W_down[l].rearrange("(h s j b) c -> h b s j c", h=2, j=4, b=2)[h, b],
+                        )
             raws[i] = raw
 
         load_unit(0)
@@ -74,6 +81,7 @@ def tile_npertokenswishglu_kernel(tc, x, W_gate, W_up, W_down, s_u, s_v, out):
         x_sb = const.tile([P, L * D], BF16, name="x_sb")
         nc.sync.dma_start(out=x_sb[:].rearrange("p (l d) -> p l d", l=L), in_=x)
         load_unit(1)
+        load_gains()
         load_unit(2)
         load_unit(3)
 
@@ -142,9 +150,9 @@ def tile_npertokenswishglu_kernel(tc, x, W_gate, W_up, W_down, s_u, s_v, out):
             if mat < 2:
                 rnb = spread(rns[i], 4 * half)
                 rv = raws[i][:].rearrange("p (j c) -> p j c", j=4)[:, :, 512 * half : 512 * (half + 1)]
-                rv = rv.rearrange("p j (m a e) -> p m a e j", a=2, e=2)
-                gv = dst.rearrange("p (a e m j) -> p m a e j", a=2, e=2, j=4)
-                bv = rnb[:].rearrange("p (e m a) -> p m a e", e=2, a=2).unsqueeze(4).to_broadcast([P, P, 2, 2, 4])
+                rv = rv.rearrange("p j (s t b) -> p s t b j", t=4, b=2)
+                gv = dst.rearrange("p (t s b j) -> p s t b j", t=4, b=2, j=4)
+                bv = rnb[:].rearrange("p (b s t) -> p s t b", b=2, t=4).unsqueeze(4).to_broadcast([P, 64, 4, 2, 4])
             else:
                 if half == 0:
                     rnbs[i] = spread(rns[i], 0)
@@ -237,8 +245,17 @@ def tile_npertokenswishglu_kernel(tc, x, W_gate, W_up, W_down, s_u, s_v, out):
             )
         us = const.tile([P, 8], F32, name="us")
         vs = const.tile([P, 8], F32, name="vs")
-        nc.scalar.activation(out=us[:], in_=su_raw[:], func=ACT.Abs)
-        nc.scalar.activation(out=vs[:], in_=sv_raw[:], func=ACT.Abs, scale=math.sqrt(D))
+        par = const.tile([P, 2], F32, name="par")
+        for b in range(2):
+            nc.vector.tensor_reduce(out=par[:, b : b + 1], in_=ident[:, b:P:2], op=ALU.add, axis=mybir.AxisListType.X)
+        even = const.tile([P, 16], F32, name="even")
+        own = const.tile([P, 16], F32, name="own")
+        nc.vector.tensor_scalar(out=even[:], in0=gains_raw[:, 0:32:2], scalar1=par[:, 0:1], scalar2=None, op0=ALU.mult)
+        nc.vector.scalar_tensor_tensor(
+            out=own[:], in0=gains_raw[:, 1:32:2], scalar=par[:, 1:2], in1=even[:], op0=ALU.mult, op1=ALU.add
+        )
+        nc.scalar.activation(out=vs[:], in_=own[:, 0:8], func=ACT.Abs, scale=math.sqrt(D))
+        nc.scalar.activation(out=us[:], in_=own[:, 8:16], func=ACT.Abs)
         x_codes = const.tile([P, L * P], U32, name="x_codes", align_bytes=64)
         x_scales = const.tile([P, L * P], U8, name="x_scales", align_bytes=64)
 

@@ -170,14 +170,14 @@ def tile_npertokenswishglu_kernel(tc, x, W_gate, W_up, W_down, s_u, s_v, out):
         uv = {}
         hgs = {}
 
-        def stage1(l, g):
-            u_ps = psum.tile([P, 4, P], UV_DT, name="u_ps", tag="uv", bufs=2)
-            v_ps = psum.tile([P, 4, P], UV_DT, name="v_ps", tag="uv", bufs=2)
+        def stage1(l):
+            v_ps = psum.tile([P, 8, P], UV_DT, name="v_ps", tag="v_ps", bufs=1)
+            u_ps = psum.tile([P, 8, P], UV_DT, name="u_ps", tag="u_ps", bufs=1)
             for dst, i in ((v_ps, 3 * l + 1), (u_ps, 3 * l)):
-                for t in range(4):
-                    cols = slice(512 * g + 128 * t, 512 * g + 128 * (t + 1))
+                for gt in range(8):
+                    cols = slice(128 * gt, 128 * (gt + 1))
                     nc.tensor.matmul_mx(
-                        out=dst[:, t, :],
+                        out=dst[:, gt, :],
                         lhsT=codes[i][:, cols].bitcast(FP8X4),
                         lhsT_scale=scales[i][:, cols],
                         rhs=x_codes[:, 128 * l : 128 * (l + 1)].bitcast(FP8X4),
@@ -185,23 +185,25 @@ def tile_npertokenswishglu_kernel(tc, x, W_gate, W_up, W_down, s_u, s_v, out):
                         start=True,
                         stop=True,
                     )
-            s1 = ep.tile([P, 4, P], F32, name="s1", tag="s1")
-            for t in range(4):
-                nc.scalar.activation(out=s1[:, t, :], in_=v_ps[:, t, :], func=ACT.Silu, scale=vs[:, 4 * g + t : 4 * g + t + 1])
-            uv[(l, g)] = (u_ps, s1)
+            s1 = ep.tile([P, 8, P], F32, name="s1", tag="s1")
+            for gt in range(8):
+                nc.scalar.activation(out=s1[:, gt, :], in_=v_ps[:, gt, :], func=ACT.Silu, scale=vs[:, gt : gt + 1])
+            uv[l] = (u_ps, s1)
 
-        def hidden(l, g):
-            u_ps, s1 = uv[(l, g)]
-            h_t = ep.tile([P, 4, P], BF16, name="h_t", tag="h_t")
-            for t in range(4):
+        def hidden(l):
+            u_ps, s1 = uv[l]
+            h_t = ep.tile([P, 8, P], BF16, name="h_t", tag="h_t")
+            for gt in range(8):
                 nc.vector.scalar_tensor_tensor(
-                    out=h_t[:, t, :], in0=u_ps[:, t, :], scalar=us[:, 4 * g + t : 4 * g + t + 1], in1=s1[:, t, :],
+                    out=h_t[:, gt, :], in0=u_ps[:, gt, :], scalar=us[:, gt : gt + 1], in1=s1[:, gt, :],
                     op0=ALU.mult, op1=ALU.mult,
                 )
-            nc.scalar.copy(
-                out=hgs[l][:, 512 * g : 512 * (g + 1)].rearrange("p (n t) -> p n t", t=4),
-                in_=h_t[:].rearrange("p t n -> p n t"),
-            )
+            hgs[l] = ep.tile([P, 1024], BF16, name="hg", tag="hg", align_bytes=64)
+            for g in range(2):
+                nc.scalar.copy(
+                    out=hgs[l][:, 512 * g : 512 * (g + 1)].rearrange("p (n t) -> p n t", t=4),
+                    in_=h_t[:, 4 * g : 4 * (g + 1), :].rearrange("p t n -> p n t"),
+                )
 
         def down(l):
             i = 3 * l + 2
@@ -265,26 +267,25 @@ def tile_npertokenswishglu_kernel(tc, x, W_gate, W_up, W_down, s_u, s_v, out):
         with tc.manual_schedule(engines={mybir.EngineType.DVE}):
             for l in range(L):
                 ig, iu, idn = 3 * l, 3 * l + 1, 3 * l + 2
-                hgs[l] = ep.tile([P, 1024], BF16, name="hg", tag="hg", align_bytes=64)
                 prefetch(ig)
                 scale(ig, 0)
                 if l > 0:
-                    down(l - 1)
+                    quantise(idn - 3, 0, 4096)
+                    hidden(l - 1)
                 scale(ig, 1)
                 prefetch(iu)
                 scale(iu, 0)
                 quantise(ig, 0, 4096)
                 if l == 0:
                     nc.vector.quantize_mx(out=x_codes[:].bitcast(FP8X4), scales=x_scales[:], in_=xg[:])
+                else:
+                    down(l - 1)
                 scale(iu, 1)
-                quantise(iu, 0, 2048)
-                stage1(l, 0)
-                quantise(iu, 2048, 4096)
                 prefetch(idn)
                 scale(idn, 0)
-                hidden(l, 0)
-                stage1(l, 1)
+                quantise(iu, 0, 4096)
+                stage1(l)
                 scale(idn, 1)
-                hidden(l, 1)
-                quantise(idn, 0, 4096)
+            quantise(3 * L - 1, 0, 4096)
+            hidden(L - 1)
             down(L - 1)

@@ -97,7 +97,7 @@ def tile_npertokenswishglu_kernel(tc, x, W_gate, W_up, W_down, s_u, s_v, out):
             nsq = small.tile([P, 8], F32, name="nsq", tag="nsq")
             rn = small.tile([P, 8], F32, name="rn", tag="rn")
             for bank in range(4):
-                wt = psum.tile([P, 4, P], F32, name="wt", tag="wt", bufs=3)
+                wt = psum.tile([P, 4, P], F32, name="wt", tag="wt", bufs=4)
                 hi, lo = divmod(bank, 2)
                 for j in range(4):
                     if mat < 2:
@@ -172,7 +172,7 @@ def tile_npertokenswishglu_kernel(tc, x, W_gate, W_up, W_down, s_u, s_v, out):
 
         def stage1(l):
             v_ps = psum.tile([P, 8, P], UV_DT, name="v_ps", tag="v_ps", bufs=1)
-            u_ps = psum.tile([P, 8, P], UV_DT, name="u_ps", tag="u_ps", bufs=1)
+            u_ps = psum.tile([P, 8, P], UV_DT, name="u_ps", tag="uo", bufs=1)
             for dst, i in ((v_ps, 3 * l + 1), (u_ps, 3 * l)):
                 for gt in range(8):
                     cols = slice(128 * gt, 128 * (gt + 1))
@@ -210,7 +210,7 @@ def tile_npertokenswishglu_kernel(tc, x, W_gate, W_up, W_down, s_u, s_v, out):
             h_codes = ep.tile([P, 256], U32, name="h_codes", tag="h_codes", align_bytes=64)
             h_scales = ep.tile([P, 256], U8, name="h_scales", tag="h_scales", align_bytes=64)
             nc.vector.quantize_mx(out=h_codes[:].bitcast(FP8X4), scales=h_scales[:], in_=hgs[l][:])
-            o_ps = psum.tile([P, 512], F32, name="o_ps", tag="o", bufs=1)
+            o_ps = psum.tile([P, 512], F32, name="o_ps", tag="uo", bufs=1)
             for g in range(2):
                 nc.tensor.matmul_mx(
                     out=o_ps[:],
@@ -236,7 +236,7 @@ def tile_npertokenswishglu_kernel(tc, x, W_gate, W_up, W_down, s_u, s_v, out):
         xg = const.tile([P, L * D], BF16, name="xg", align_bytes=64)
         xgw = xg[:].bitcast(F32)
         for lp in range(L // 2):
-            xt = psum.tile([P, 4, P], F32, name="xt", tag="wt", bufs=3)
+            xt = psum.tile([P, 4, P], F32, name="xt", tag="wt", bufs=4)
             for l2 in range(2):
                 for u in range(2):
                     l = 2 * lp + l2

@@ -127,6 +127,15 @@ def tile_npertokenswishglu_kernel(tc, x, W_gate, W_up, W_down, s_u, s_v, out):
                 nc.tensor.transpose(rnb[:, 128 * k : 128 * (k + 1)], rn[:, c0 + k : c0 + k + 1].to_broadcast([P, P]), ident[:])
             return rnb
 
+        def spread_natural(rn):
+            rnb = psum.tile([P, 512], F32, name="rnb", tag="rnb", bufs=2)
+            for k in range(4):
+                e, hi = divmod(k, 2)
+                nc.tensor.transpose(
+                    rnb[:, 256 * hi + e : 256 * (hi + 1) : 2], rn[:, k : k + 1].to_broadcast([P, P]), ident[:]
+                )
+            return rnb
+
         rns = {}
         grps = {}
         codes = {}
@@ -155,11 +164,11 @@ def tile_npertokenswishglu_kernel(tc, x, W_gate, W_up, W_down, s_u, s_v, out):
                 bv = rnb[:].rearrange("p (b s t) -> p s t b", b=2, t=4).unsqueeze(4).to_broadcast([P, 64, 4, 2, 4])
             else:
                 if half == 0:
-                    rnbs[i] = spread(rns[i], 0)
+                    rnbs[i] = spread_natural(rns[i])
                 rnb = rnbs[i]
-                rv = chunk.rearrange("p (j c e) -> p c e j", j=4, e=2)
-                gv = dst.rearrange("p (c e j) -> p c e j", e=2, j=4)
-                bv = rnb[:].rearrange("p (e c) -> p c e", e=2).unsqueeze(3).to_broadcast([P, 256, 2, 4])
+                rv = chunk.rearrange("p (j x i) -> p x j i", j=4, i=4)
+                gv = dst.rearrange("p (x i j) -> p x j i", i=4, j=4)
+                bv = rnb[:].rearrange("p (x i) -> p x i", i=4).unsqueeze(2).to_broadcast([P, 128, 4, 4])
             nc.vector.tensor_tensor(out=gv, in0=rv, in1=bv, op=ALU.mult)
 
         def quantise(i, lo, hi):

@@ -19,15 +19,32 @@ P = 128
 EPS_SQ = 1e-24
 UV_DT = BF16
 LEAD = 2
+PB = 4
+UB = 3 * PB
+X_COPY_AT = 4
+X_QUANT_AT = 6
+
+
+def unit_order():
+    units = []
+    for b in range(L // PB):
+        for l in range(PB * b, PB * (b + 1)):
+            units.append((l, 0))
+            units.append((l, 1))
+        for l in range(PB * b, PB * (b + 1)):
+            units.append((l, 2))
+    return units
 
 
 def tile_npertokenswishglu_kernel(tc, x, W_gate, W_up, W_down, s_u, s_v, out):
     nc = tc.nc
+    units = unit_order()
+    NU = len(units)
     with ExitStack() as ctx:
         const = ctx.enter_context(tc.tile_pool(name="const", bufs=1))
         rawp = ctx.enter_context(tc.tile_pool(name="rawp", bufs=6))
         grpp = ctx.enter_context(tc.tile_pool(name="grpp", bufs=3))
-        codep = ctx.enter_context(tc.tile_pool(name="codep", bufs=5))
+        codep = ctx.enter_context(tc.tile_pool(name="codep", bufs=2 * PB))
         small = ctx.enter_context(tc.tile_pool(name="small", bufs=6))
         junkp = ctx.enter_context(tc.tile_pool(name="junkp", bufs=2))
         ep = ctx.enter_context(tc.tile_pool(name="ep", bufs=2))
@@ -53,7 +70,7 @@ def tile_npertokenswishglu_kernel(tc, x, W_gate, W_up, W_down, s_u, s_v, out):
         raws = {}
 
         def load_unit(i):
-            l, mat = divmod(i, 3)
+            l, mat = units[i]
             raw = rawp.tile([P, 4096], BF16, name="raw", tag="raw")
             if i == 0:
                 for b in range(4):
@@ -77,13 +94,12 @@ def tile_npertokenswishglu_kernel(tc, x, W_gate, W_up, W_down, s_u, s_v, out):
             raws[i] = raw
 
         load_unit(0)
-
-        x_sb = const.tile([P, L * D], BF16, name="x_sb")
-        nc.sync.dma_start(out=x_sb[:].rearrange("p (l d) -> p l d", l=L), in_=x)
         load_unit(1)
         load_gains()
         load_unit(2)
         load_unit(3)
+        x_sb = const.tile([P, L * D], BF16, name="x_sb")
+        nc.sync.dma_start(out=x_sb[:].rearrange("p (l d) -> p l d", l=L), in_=x)
 
         def rsqrt_cols(dst, src):
             n = src.shape[1]
@@ -92,7 +108,7 @@ def tile_npertokenswishglu_kernel(tc, x, W_gate, W_up, W_down, s_u, s_v, out):
             nc.gpsimd.tensor_tensor(out=dst, in0=clamped[:, 0:n], in1=mhalf[:, 0:n], op=ALU.pow)
 
         def norms(i):
-            mat = i % 3
+            mat = units[i][1]
             words = raws[i][:].bitcast(F32)
             nsq = small.tile([P, 8], F32, name="nsq", tag="nsq")
             rn = small.tile([P, 8], F32, name="rn", tag="rn")
@@ -143,17 +159,21 @@ def tile_npertokenswishglu_kernel(tc, x, W_gate, W_up, W_down, s_u, s_v, out):
         rnbs = {}
 
         def prefetch(i):
-            if 4 <= i + 4 < 3 * L:
+            if i + 4 < NU:
                 load_unit(i + 4)
-            if LEAD <= i + LEAD < 3 * L:
+            if i + LEAD < NU:
                 rns[i + LEAD] = norms(i + LEAD)
 
         def scale(i, half):
-            mat = i % 3
+            mat = units[i][1]
             if half == 0:
                 grps[i] = grpp.tile([P, 4096], BF16, name="grp", tag="grp", align_bytes=64)
-                codes[i] = codep.tile([P, 1024], U32, name="wcodes", tag="wcodes", align_bytes=64)
-                scales[i] = codep.tile([P, 1024], U8, name="wscales", tag="wscales", align_bytes=64)
+                if mat < 2:
+                    codes[i] = codep.tile([P, 1024], U32, name="gucodes", tag="gucodes", align_bytes=64)
+                    scales[i] = codep.tile([P, 1024], U8, name="guscales", tag="guscales", align_bytes=64)
+                else:
+                    codes[i] = codep.tile([P, 1024], U32, name="dcodes", tag="dcodes", bufs=PB, align_bytes=64)
+                    scales[i] = codep.tile([P, 1024], U8, name="dscales", tag="dscales", bufs=PB, align_bytes=64)
             chunk = raws[i][:, 2048 * half : 2048 * (half + 1)] if mat == 2 else None
             dst = grps[i][:, 2048 * half : 2048 * (half + 1)]
             if mat < 2:
@@ -171,22 +191,24 @@ def tile_npertokenswishglu_kernel(tc, x, W_gate, W_up, W_down, s_u, s_v, out):
                 bv = rnb[:].rearrange("p (x i) -> p x i", i=4).unsqueeze(2).to_broadcast([P, 128, 4, 4])
             nc.vector.tensor_tensor(out=gv, in0=rv, in1=bv, op=ALU.mult)
 
-        def quantise(i, lo, hi):
-            nc.vector.quantize_mx(
-                out=codes[i][:, lo // 4 : hi // 4].bitcast(FP8X4), scales=scales[i][:, lo // 4 : hi // 4], in_=grps[i][:, lo:hi]
-            )
+        def quantise(i):
+            nc.vector.quantize_mx(out=codes[i][:].bitcast(FP8X4), scales=scales[i][:], in_=grps[i][:])
 
-        uv = {}
+        s1s = {}
+        u_pss = {}
+        h_ts = {}
         hgs = {}
+        h_codes = {}
+        h_scales = {}
 
-        def stage1(l):
-            v_ps = psum.tile([P, 8, P], UV_DT, name="v_ps", tag="v_ps", bufs=1)
-            u_ps = psum.tile([P, 8, P], UV_DT, name="u_ps", tag="uo", bufs=1)
-            for dst, i in ((v_ps, 3 * l + 1), (u_ps, 3 * l)):
-                for gt in range(8):
-                    cols = slice(128 * gt, 128 * (gt + 1))
+        def passes(dst, b, r, mat):
+            for s2 in range(2):
+                cols = slice(128 * (2 * r + s2), 128 * (2 * r + s2 + 1))
+                for l4 in range(PB):
+                    l = PB * b + l4
+                    i = UB * b + 2 * l4 + mat
                     nc.tensor.matmul_mx(
-                        out=dst[:, gt, :],
+                        out=dst[:, s2, l4, :],
                         lhsT=codes[i][:, cols].bitcast(FP8X4),
                         lhsT_scale=scales[i][:, cols],
                         rhs=x_codes[:, 128 * l : 128 * (l + 1)].bitcast(FP8X4),
@@ -194,37 +216,56 @@ def tile_npertokenswishglu_kernel(tc, x, W_gate, W_up, W_down, s_u, s_v, out):
                         start=True,
                         stop=True,
                     )
-            s1 = ep.tile([P, 8, P], F32, name="s1", tag="s1")
-            for gt in range(8):
-                nc.scalar.activation(out=s1[:, gt, :], in_=v_ps[:, gt, :], func=ACT.Silu, scale=vs[:, gt : gt + 1])
-            uv[l] = (u_ps, s1)
 
-        def hidden(l):
-            u_ps, s1 = uv[l]
-            h_t = ep.tile([P, 8, P], BF16, name="h_t", tag="h_t")
-            for gt in range(8):
+        def v_round(b, r):
+            v_ps = psum.tile([P, 2, PB, P], UV_DT, name="v_ps", tag="v_ps", bufs=1)
+            passes(v_ps, b, r, 1)
+            s1 = ep.tile([P, 2, PB * P], F32, name="s1", tag="s1")
+            for s2 in range(2):
+                gt = 2 * r + s2
+                nc.scalar.activation(
+                    out=s1[:, s2, :], in_=v_ps[:, s2].rearrange("p l n -> p (l n)"), func=ACT.Silu, scale=vs[:, gt : gt + 1]
+                )
+            s1s[r] = s1
+
+        def u_round(b, r):
+            u_ps = psum.tile([P, 2, PB, P], UV_DT, name="u_ps", tag="uo", bufs=1)
+            passes(u_ps, b, r, 0)
+            u_pss[r] = u_ps
+
+        def products(b, r):
+            if r == 0:
+                h_ts[b] = ep.tile([P, 8, PB * P], BF16, name="h_t", tag="h_t", bufs=1)
+            for s2 in range(2):
+                gt = 2 * r + s2
                 nc.vector.scalar_tensor_tensor(
-                    out=h_t[:, gt, :], in0=u_ps[:, gt, :], scalar=us[:, gt : gt + 1], in1=s1[:, gt, :],
-                    op0=ALU.mult, op1=ALU.mult,
+                    out=h_ts[b][:, gt, :], in0=u_pss[r][:, s2].rearrange("p l n -> p (l n)"), scalar=us[:, gt : gt + 1],
+                    in1=s1s[r][:, s2, :], op0=ALU.mult, op1=ALU.mult,
                 )
-            hgs[l] = ep.tile([P, 1024], BF16, name="hg", tag="hg", align_bytes=64)
-            for g in range(2):
-                nc.scalar.copy(
-                    out=hgs[l][:, 512 * g : 512 * (g + 1)].rearrange("p (n t) -> p n t", t=4),
-                    in_=h_t[:, 4 * g : 4 * (g + 1), :].rearrange("p t n -> p n t"),
-                )
+
+        def interleave(b, g):
+            if g == 0:
+                hgs[b] = ep.tile([P, PB * 1024], BF16, name="hg", tag="hg", bufs=1, align_bytes=64)
+            dst = hgs[b][:].rearrange("p (l g n t) -> p g l n t", l=PB, g=2, t=4)
+            src = h_ts[b][:, 4 * g : 4 * (g + 1), :].rearrange("p t (l n) -> p l n t", l=PB)
+            for pair in range(PB // 2):
+                nc.scalar.copy(out=dst[:, g, 2 * pair : 2 * pair + 2], in_=src[:, 2 * pair : 2 * pair + 2])
+
+        def quantise_h(b):
+            h_codes[b] = ep.tile([P, PB * 256], U32, name="h_codes", tag="h_codes", bufs=1, align_bytes=64)
+            h_scales[b] = ep.tile([P, PB * 256], U8, name="h_scales", tag="h_scales", bufs=1, align_bytes=64)
+            nc.vector.quantize_mx(out=h_codes[b][:].bitcast(FP8X4), scales=h_scales[b][:], in_=hgs[b][:])
 
         def down(l):
-            i = 3 * l + 2
-            h_codes = ep.tile([P, 256], U32, name="h_codes", tag="h_codes", align_bytes=64)
-            h_scales = ep.tile([P, 256], U8, name="h_scales", tag="h_scales", align_bytes=64)
-            nc.vector.quantize_mx(out=h_codes[:].bitcast(FP8X4), scales=h_scales[:], in_=hgs[l][:])
-            o_ps = psum.tile([P, 512], F32, name="o_ps", tag="uo", bufs=1)
+            b, l4 = divmod(l, PB)
+            i = UB * b + 2 * PB + l4
+            o_ps = psum.tile([P, 512], F32, name="o_ps", tag=("uo" if l4 % 2 == 0 else "v_ps"), bufs=1)
             for g in range(2):
+                cols = slice(256 * l4 + 128 * g, 256 * l4 + 128 * (g + 1))
                 nc.tensor.matmul_mx(
                     out=o_ps[:],
-                    lhsT=h_codes[:, 128 * g : 128 * (g + 1)].bitcast(FP8X4),
-                    lhsT_scale=h_scales[:, 128 * g : 128 * (g + 1)],
+                    lhsT=h_codes[b][:, cols].bitcast(FP8X4),
+                    lhsT_scale=h_scales[b][:, cols],
                     rhs=codes[i][:, 512 * g : 512 * (g + 1)].bitcast(FP8X4),
                     rhs_scale=scales[i][:, 512 * g : 512 * (g + 1)],
                     start=(g == 0),
@@ -241,19 +282,6 @@ def tile_npertokenswishglu_kernel(tc, x, W_gate, W_up, W_down, s_u, s_v, out):
 
         rns[0] = norms(0)
 
-        xw = x_sb[:].bitcast(F32)
-        xg = const.tile([P, L * D], BF16, name="xg", align_bytes=64)
-        xgw = xg[:].bitcast(F32)
-        for lp in range(L // 2):
-            xt = psum.tile([P, 4, P], F32, name="xt", tag="wt", bufs=4)
-            for l2 in range(2):
-                for u in range(2):
-                    l = 2 * lp + l2
-                    nc.tensor.transpose(xt[:, 2 * l2 + u, :], xw[:, 256 * l + u : 256 * (l + 1) : 2], ident[:])
-            nc.scalar.copy(
-                out=xgw[:, 512 * lp : 512 * (lp + 1)].rearrange("p (a n u) -> p a n u", a=2, u=2),
-                in_=xt[:].rearrange("p (a u) n -> p a n u", a=2),
-            )
         us = const.tile([P, 8], F32, name="us")
         vs = const.tile([P, 8], F32, name="vs")
         par = const.tile([P, 2], F32, name="par")
@@ -267,34 +295,63 @@ def tile_npertokenswishglu_kernel(tc, x, W_gate, W_up, W_down, s_u, s_v, out):
         )
         nc.scalar.activation(out=vs[:], in_=own[:, 0:8], func=ACT.Abs, scale=math.sqrt(D))
         nc.scalar.activation(out=us[:], in_=own[:, 8:16], func=ACT.Abs)
+        xg = const.tile([P, L * D], BF16, name="xg", align_bytes=64)
         x_codes = const.tile([P, L * P], U32, name="x_codes", align_bytes=64)
         x_scales = const.tile([P, L * P], U8, name="x_scales", align_bytes=64)
+
+        def turn_x():
+            xw = x_sb[:].bitcast(F32)
+            xgw = xg[:].bitcast(F32)
+            for lp in range(L // 2):
+                xt = psum.tile([P, 4, P], F32, name="xt", tag="wt", bufs=4)
+                for l2 in range(2):
+                    for u in range(2):
+                        l = 2 * lp + l2
+                        nc.tensor.transpose(xt[:, 2 * l2 + u, :], xw[:, 256 * l + u : 256 * (l + 1) : 2], ident[:])
+                nc.scalar.copy(
+                    out=xgw[:, 512 * lp : 512 * (lp + 1)].rearrange("p (a n u) -> p a n u", a=2, u=2),
+                    in_=xt[:].rearrange("p (a u) n -> p a n u", a=2),
+                )
 
         for i in range(1, LEAD):
             rns[i] = norms(i)
 
         with tc.manual_schedule(engines={mybir.EngineType.DVE}):
-            for l in range(L):
-                ig, iu, idn = 3 * l, 3 * l + 1, 3 * l + 2
-                prefetch(ig)
-                scale(ig, 0)
-                if l > 0:
-                    quantise(idn - 3, 0, 4096)
-                    hidden(l - 1)
-                scale(ig, 1)
-                prefetch(iu)
-                scale(iu, 0)
-                quantise(ig, 0, 4096)
-                if l == 0:
+            for i in range(NU):
+                b, k = divmod(i, UB)
+                if i == X_COPY_AT:
+                    turn_x()
+                prefetch(i)
+                scale(i, 0)
+                if i > 0:
+                    quantise(i - 1)
+                if i == X_QUANT_AT:
                     nc.vector.quantize_mx(out=x_codes[:].bitcast(FP8X4), scales=x_scales[:], in_=xg[:])
-                else:
-                    down(l - 1)
-                scale(iu, 1)
-                prefetch(idn)
-                scale(idn, 0)
-                quantise(iu, 0, 4096)
-                stage1(l)
-                scale(idn, 1)
-            quantise(3 * L - 1, 0, 4096)
-            hidden(L - 1)
+                if k == 0 and b > 0:
+                    down(PB * b - 1)
+                if k == 2 * PB:
+                    v_round(b, 0)
+                    u_round(b, 0)
+                    v_round(b, 1)
+                if k == 2 * PB + 1:
+                    products(b, 1)
+                    interleave(b, 0)
+                    u_round(b, 2)
+                    v_round(b, 3)
+                if k == 2 * PB + 2:
+                    products(b, 3)
+                    interleave(b, 1)
+                if k == 2 * PB + 3:
+                    quantise_h(b)
+                    for l4 in range(PB - 1):
+                        down(PB * b + l4)
+                scale(i, 1)
+                if k == 2 * PB:
+                    products(b, 0)
+                    u_round(b, 1)
+                    v_round(b, 2)
+                if k == 2 * PB + 1:
+                    products(b, 2)
+                    u_round(b, 3)
+            quantise(NU - 1)
             down(L - 1)

@@ -21,6 +21,7 @@ UV_DT = BF16
 LEAD = 2
 PB = 4
 UB = 3 * PB
+PS_BUFS = {"wt": 3, "rnb": 2, "v_ps": 2, "uo": 1}
 X_COPY_AT = 4
 X_QUANT_AT = 6
 
@@ -112,8 +113,12 @@ def tile_npertokenswishglu_kernel(tc, x, W_gate, W_up, W_down, s_u, s_v, out):
             words = raws[i][:].bitcast(F32)
             nsq = small.tile([P, 8], F32, name="nsq", tag="nsq")
             rn = small.tile([P, 8], F32, name="rn", tag="rn")
+            k = i % UB
             for bank in range(4):
-                wt = psum.tile([P, 4, P], F32, name="wt", tag="wt", bufs=4)
+                tag = "wt"
+                if 3 <= k <= 2 * PB - 1 and bank % 2 == 1:
+                    tag = "v_ps" if bank == 1 else "uo"
+                wt = psum.tile([P, 4, P], F32, name="wt", tag=tag, bufs=PS_BUFS[tag])
                 hi, lo = divmod(bank, 2)
                 for j in range(4):
                     if mat < 2:
@@ -218,7 +223,7 @@ def tile_npertokenswishglu_kernel(tc, x, W_gate, W_up, W_down, s_u, s_v, out):
                     )
 
         def v_round(b, r):
-            v_ps = psum.tile([P, 2, PB, P], UV_DT, name="v_ps", tag="v_ps", bufs=1)
+            v_ps = psum.tile([P, 2, PB, P], UV_DT, name="v_ps", tag="v_ps", bufs=PS_BUFS["v_ps"])
             passes(v_ps, b, r, 1)
             s1 = ep.tile([P, 2, PB * P], F32, name="s1", tag="s1")
             for s2 in range(2):
@@ -259,7 +264,8 @@ def tile_npertokenswishglu_kernel(tc, x, W_gate, W_up, W_down, s_u, s_v, out):
         def down(l):
             b, l4 = divmod(l, PB)
             i = UB * b + 2 * PB + l4
-            o_ps = psum.tile([P, 512], F32, name="o_ps", tag=("uo" if l4 % 2 == 0 else "v_ps"), bufs=1)
+            tag = "uo" if l4 % 2 == 0 else "v_ps"
+            o_ps = psum.tile([P, 512], F32, name="o_ps", tag=tag, bufs=PS_BUFS[tag])
             for g in range(2):
                 cols = slice(256 * l4 + 128 * g, 256 * l4 + 128 * (g + 1))
                 nc.tensor.matmul_mx(
@@ -303,7 +309,7 @@ def tile_npertokenswishglu_kernel(tc, x, W_gate, W_up, W_down, s_u, s_v, out):
             xw = x_sb[:].bitcast(F32)
             xgw = xg[:].bitcast(F32)
             for lp in range(L // 2):
-                xt = psum.tile([P, 4, P], F32, name="xt", tag="wt", bufs=4)
+                xt = psum.tile([P, 4, P], F32, name="xt", tag="wt", bufs=PS_BUFS["wt"])
                 for l2 in range(2):
                     for u in range(2):
                         l = 2 * lp + l2

@@ -196,8 +196,10 @@ def tile_npertokenswishglu_kernel(tc, x, W_gate, W_up, W_down, s_u, s_v, out):
                 bv = rnb[:].rearrange("p (x i) -> p x i", i=4).unsqueeze(2).to_broadcast([P, 128, 4, 4])
             nc.vector.tensor_tensor(out=gv, in0=rv, in1=bv, op=ALU.mult)
 
-        def quantise(i):
-            nc.vector.quantize_mx(out=codes[i][:].bitcast(FP8X4), scales=scales[i][:], in_=grps[i][:])
+        def quantise(i, lo=0, hi=4096):
+            nc.vector.quantize_mx(
+                out=codes[i][:, lo // 4 : hi // 4].bitcast(FP8X4), scales=scales[i][:, lo // 4 : hi // 4], in_=grps[i][:, lo:hi]
+            )
 
         s1s = {}
         u_pss = {}
@@ -265,6 +267,8 @@ def tile_npertokenswishglu_kernel(tc, x, W_gate, W_up, W_down, s_u, s_v, out):
             b, l4 = divmod(l, PB)
             i = UB * b + 2 * PB + l4
             tag = "uo" if l4 % 2 == 0 else "v_ps"
+            if b == L // PB - 1 and l4 == 2:
+                tag = "wt"
             o_ps = psum.tile([P, 512], F32, name="o_ps", tag=tag, bufs=PS_BUFS[tag])
             for g in range(2):
                 cols = slice(256 * l4 + 128 * g, 256 * l4 + 128 * (g + 1))
@@ -351,6 +355,8 @@ def tile_npertokenswishglu_kernel(tc, x, W_gate, W_up, W_down, s_u, s_v, out):
                     quantise_h(b)
                     for l4 in range(PB - 1):
                         down(PB * b + l4)
+                if i == NU - 1:
+                    quantise(i, 0, 2048)
                 scale(i, 1)
                 if k == 2 * PB:
                     products(b, 0)
@@ -359,5 +365,5 @@ def tile_npertokenswishglu_kernel(tc, x, W_gate, W_up, W_down, s_u, s_v, out):
                 if k == 2 * PB + 1:
                     products(b, 2)
                     u_round(b, 3)
-            quantise(NU - 1)
+            quantise(NU - 1, 2048, 4096)
             down(L - 1)

@@ -333,6 +333,10 @@ def tile_npertokenswishglu_kernel(tc, x, W_gate, W_up, W_down, s_u, s_v, out):
                     turn_x()
                 prefetch(i)
                 scale(i, 0)
+                if i == NU - 1:
+                    quantise_h(b)
+                    down(PB * b)
+                    down(PB * b + 1)
                 if i > 0:
                     quantise(i - 1)
                 if i == X_QUANT_AT:
@@ -351,7 +355,9 @@ def tile_npertokenswishglu_kernel(tc, x, W_gate, W_up, W_down, s_u, s_v, out):
                 if k == 2 * PB + 2:
                     products(b, 3)
                     interleave(b, 1)
-                if k == 2 * PB + 3:
+                if i == NU - 1:
+                    down(PB * b + 2)
+                elif k == 2 * PB + 3:
                     quantise_h(b)
                     for l4 in range(PB - 1):
                         down(PB * b + l4)

from contextlib import ExitStack
import math

import concourse.mybir as mybir
from concourse.masks import make_identity

B, L, D, F = 128, 8, 512, 1024
FLOPS = 2 * B * L * (2 * D * F + F * D)

F32 = mybir.dt.float32
BF16 = mybir.dt.bfloat16
U32 = mybir.dt.uint32
U8 = mybir.dt.uint8
FP8X4 = mybir.dt.float8_e4m3fn_x4
ACT = mybir.ActivationFunctionType
ALU = mybir.AluOpType

P = 128
EPS_SQ = 1e-24
UV_DT = BF16
LEAD = 2
PB = 4
UB = 3 * PB
PS_BUFS = {"wt": 3, "rnb": 2, "v_ps": 2, "uo": 1}
X_COPY_AT = 4
X_QUANT_AT = 6


def unit_order():
    units = []
    for b in range(L // PB):
        for l in range(PB * b, PB * (b + 1)):
            units.append((l, 0))
            units.append((l, 1))
        for l in range(PB * b, PB * (b + 1)):
            units.append((l, 2))
    return units


def tile_npertokenswishglu_kernel(tc, x, W_gate, W_up, W_down, s_u, s_v, out):
    nc = tc.nc
    units = unit_order()
    NU = len(units)
    with ExitStack() as ctx:
        const = ctx.enter_context(tc.tile_pool(name="const", bufs=1))
        rawp = ctx.enter_context(tc.tile_pool(name="rawp", bufs=6))
        grpp = ctx.enter_context(tc.tile_pool(name="grpp", bufs=3))
        codep = ctx.enter_context(tc.tile_pool(name="codep", bufs=2 * PB))
        small = ctx.enter_context(tc.tile_pool(name="small", bufs=6))
        junkp = ctx.enter_context(tc.tile_pool(name="junkp", bufs=2))
        ep = ctx.enter_context(tc.tile_pool(name="ep", bufs=2))
        psum = ctx.enter_context(tc.psum_pool(name="psum", bufs=1))

        ident = const.tile([P, P], F32, name="ident")
        make_identity(nc, ident[:])
        mhalf = const.tile([P, 8], F32, name="mhalf")
        nc.gpsimd.memset(mhalf[:], -0.5)
        warm = const.tile([P, 1], F32, name="warm")
        nc.scalar.activation(out=warm[:], in_=mhalf[:, 0:1], func=ACT.Silu)

        gains_raw = const.tile([P, 32], BF16, name="gains_raw")

        def load_gains():
            for w, src_v in enumerate((s_v, s_u)):
                for b in range(2):
                    nc.sync.dma_start(
                        out=gains_raw[b:P:2, 16 * w : 16 * (w + 1)].rearrange("p (g k) -> p g k", g=2),
                        in_=src_v.rearrange("o (g s k) -> s (o g) k", g=2, k=8),
                    )

        raws = {}

        def load_unit(i):
            l, mat = units[i]
            raw = rawp.tile([P, 4096], BF16, name="raw", tag="raw")
            if i == 0:
                for b in range(4):
                    nc.sync.dma_start(
                        out=raw[:].rearrange("p (j c) -> p j c", j=4)[:, :, 256 * b : 256 * (b + 1)],
                        in_=W_gate[l].rearrange("(p j) c -> p j c", j=4)[:, :, 256 * b : 256 * (b + 1)],
                    )
            elif mat < 2:
                w = W_gate if mat == 0 else W_up
                nc.sync.dma_start(
                    out=raw[:].rearrange("p (j c) -> p j c", j=4),
                    in_=w[l].rearrange("(p j) c -> p j c", j=4),
                )
            else:
                for h in range(2):
                    for b in range(2):
                        nc.sync.dma_start(
                            out=raw[b:P:2, 2048 * h : 2048 * (h + 1)].rearrange("p (j c) -> p j c", j=4),
                            in_=W_down[l].rearrange("(h s j b) c -> h b s j c", h=2, j=4, b=2)[h, b],
                        )
            raws[i] = raw

        load_unit(0)
        load_unit(1)
        load_gains()
        load_unit(2)
        load_unit(3)
        x_sb = const.tile([P, L * D], BF16, name="x_sb")
        nc.sync.dma_start(out=x_sb[:].rearrange("p (l d) -> p l d", l=L), in_=x)

        def rsqrt_cols(dst, src):
            n = src.shape[1]
            clamped = small.tile([P, 8], F32, name="clamped", tag="clamped")
            nc.gpsimd.tensor_scalar(out=clamped[:, 0:n], in0=src, scalar1=EPS_SQ, scalar2=None, op0=ALU.max)
            nc.gpsimd.tensor_tensor(out=dst, in0=clamped[:, 0:n], in1=mhalf[:, 0:n], op=ALU.pow)

        def norms(i):
            mat = units[i][1]
            words = raws[i][:].bitcast(F32)
            nsq = small.tile([P, 8], F32, name="nsq", tag="nsq")
            rn = small.tile([P, 8], F32, name="rn", tag="rn")
            k = i % UB
            for bank in range(4):
                tag = "wt"
                if 3 <= k <= 2 * PB - 1 and bank % 2 == 1:
                    tag = "v_ps" if bank == 1 else "uo"
                wt = psum.tile([P, 4, P], F32, name="wt", tag=tag, bufs=PS_BUFS[tag])
                hi, lo = divmod(bank, 2)
                for j in range(4):
                    if mat < 2:
                        off = 512 * j + 128 * bank
                    else:
                        off = 1024 * lo + 256 * j + 128 * hi
                    nc.tensor.transpose(wt[:, j, :], words[:, off : off + 128], ident[:])
                halves = wt[:].rearrange("p j q -> p (j q)").bitcast(BF16).rearrange("p (n e) -> p e n", e=2)
                for e in range(2):
                    if mat < 2:
                        col = 4 * hi + 2 * e + lo
                    else:
                        col = 4 * lo + 2 * e + hi
                    junk = junkp.tile([P, 512], BF16, name="junk", tag="junk")
                    nc.scalar.activation(out=junk[:], in_=halves[:, e, :], func=ACT.Square, accum_out=nsq[:, col : col + 1])
                if mat < 2 and lo == 1:
                    rsqrt_cols(rn[:, 4 * hi : 4 * hi + 4], nsq[:, 4 * hi : 4 * hi + 4])
            if mat == 2:
                tot = small.tile([P, 4], F32, name="tot", tag="tot")
                nc.gpsimd.tensor_tensor(out=tot[:], in0=nsq[:, 0:4], in1=nsq[:, 4:8], op=ALU.add)
                rsqrt_cols(rn[:, 0:4], tot[:])
            return rn

        def spread(rn, c0):
            rnb = psum.tile([P, 512], F32, name="rnb", tag="rnb", bufs=2)
            for k in range(4):
                nc.tensor.transpose(rnb[:, 128 * k : 128 * (k + 1)], rn[:, c0 + k : c0 + k + 1].to_broadcast([P, P]), ident[:])
            return rnb

        def spread_natural(rn):
            rnb = psum.tile([P, 512], F32, name="rnb", tag="rnb", bufs=2)
            for k in range(4):
                e, hi = divmod(k, 2)
                nc.tensor.transpose(
                    rnb[:, 256 * hi + e : 256 * (hi + 1) : 2], rn[:, k : k + 1].to_broadcast([P, P]), ident[:]
                )
            return rnb

        rns = {}
        grps = {}
        codes = {}
        scales = {}
        rnbs = {}

        def prefetch(i):
            if i + 4 < NU:
                load_unit(i + 4)
            if i + LEAD < NU:
                rns[i + LEAD] = norms(i + LEAD)

        def scale(i, half):
            mat = units[i][1]
            if half == 0:
                grps[i] = grpp.tile([P, 4096], BF16, name="grp", tag="grp", align_bytes=64)
                if mat < 2:
                    codes[i] = codep.tile([P, 1024], U32, name="gucodes", tag="gucodes", align_bytes=64)
                    scales[i] = codep.tile([P, 1024], U8, name="guscales", tag="guscales", align_bytes=64)
                else:
                    codes[i] = codep.tile([P, 1024], U32, name="dcodes", tag="dcodes", bufs=PB, align_bytes=64)
                    scales[i] = codep.tile([P, 1024], U8, name="dscales", tag="dscales", bufs=PB, align_bytes=64)
            chunk = raws[i][:, 2048 * half : 2048 * (half + 1)] if mat == 2 else None
            dst = grps[i][:, 2048 * half : 2048 * (half + 1)]
            if mat < 2:
                rnb = spread(rns[i], 4 * half)
                rv = raws[i][:].rearrange("p (j c) -> p j c", j=4)[:, :, 512 * half : 512 * (half + 1)]
                rv = rv.rearrange("p j (s t b) -> p s t b j", t=4, b=2)
                gv = dst.rearrange("p (t s b j) -> p s t b j", t=4, b=2, j=4)
                bv = rnb[:].rearrange("p (b s t) -> p s t b", b=2, t=4).unsqueeze(4).to_broadcast([P, 64, 4, 2, 4])
            else:
                if half == 0:
                    rnbs[i] = spread_natural(rns[i])
                rnb = rnbs[i]
                rv = chunk.rearrange("p (j x i) -> p x j i", j=4, i=4)
                gv = dst.rearrange("p (x i j) -> p x j i", i=4, j=4)
                bv = rnb[:].rearrange("p (x i) -> p x i", i=4).unsqueeze(2).to_broadcast([P, 128, 4, 4])
            nc.vector.tensor_tensor(out=gv, in0=rv, in1=bv, op=ALU.mult)

        def quantise(i, lo=0, hi=4096):
            nc.vector.quantize_mx(
                out=codes[i][:, lo // 4 : hi // 4].bitcast(FP8X4), scales=scales[i][:, lo // 4 : hi // 4], in_=grps[i][:, lo:hi]
            )

        s1s = {}
        u_pss = {}
        h_ts = {}
        hgs = {}
        h_codes = {}
        h_scales = {}

        def passes(dst, b, r, mat):
            for s2 in range(2):
                cols = slice(128 * (2 * r + s2), 128 * (2 * r + s2 + 1))
                for l4 in range(PB):
                    l = PB * b + l4
                    i = UB * b + 2 * l4 + mat
                    nc.tensor.matmul_mx(
                        out=dst[:, s2, l4, :],
                        lhsT=codes[i][:, cols].bitcast(FP8X4),
                        lhsT_scale=scales[i][:, cols],
                        rhs=x_codes[:, 128 * l : 128 * (l + 1)].bitcast(FP8X4),
                        rhs_scale=x_scales[:, 128 * l : 128 * (l + 1)],
                        start=True,
                        stop=True,
                    )

        def v_round(b, r):
            v_ps = psum.tile([P, 2, PB, P], UV_DT, name="v_ps", tag="v_ps", bufs=PS_BUFS["v_ps"])
            passes(v_ps, b, r, 1)
            s1 = ep.tile([P, 2, PB * P], F32, name="s1", tag="s1")
            for s2 in range(2):
                gt = 2 * r + s2
                nc.scalar.activation(
                    out=s1[:, s2, :], in_=v_ps[:, s2].rearrange("p l n -> p (l n)"), func=ACT.Silu, scale=vs[:, gt : gt + 1]
                )
            s1s[r] = s1

        def u_round(b, r):
            u_ps = psum.tile([P, 2, PB, P], UV_DT, name="u_ps", tag="uo", bufs=1)
            passes(u_ps, b, r, 0)
            u_pss[r] = u_ps

        def products(b, r):
            if r == 0:
                h_ts[b] = ep.tile([P, 8, PB * P], BF16, name="h_t", tag="h_t", bufs=1)
            for s2 in range(2):
                gt = 2 * r + s2
                nc.vector.scalar_tensor_tensor(
                    out=h_ts[b][:, gt, :], in0=u_pss[r][:, s2].rearrange("p l n -> p (l n)"), scalar=us[:, gt : gt + 1],
                    in1=s1s[r][:, s2, :], op0=ALU.mult, op1=ALU.mult,
                )

        def interleave(b, g):
            if g == 0:
                hgs[b] = ep.tile([P, PB * 1024], BF16, name="hg", tag="hg", bufs=1, align_bytes=64)
            dst = hgs[b][:].rearrange("p (l g n t) -> p g l n t", l=PB, g=2, t=4)
            src = h_ts[b][:, 4 * g : 4 * (g + 1), :].rearrange("p t (l n) -> p l n t", l=PB)
            for pair in range(PB // 2):
                nc.scalar.copy(out=dst[:, g, 2 * pair : 2 * pair + 2], in_=src[:, 2 * pair : 2 * pair + 2])

        def quantise_h(b):
            h_codes[b] = ep.tile([P, PB * 256], U32, name="h_codes", tag="h_codes", bufs=1, align_bytes=64)
            h_scales[b] = ep.tile([P, PB * 256], U8, name="h_scales", tag="h_scales", bufs=1, align_bytes=64)
            nc.vector.quantize_mx(out=h_codes[b][:].bitcast(FP8X4), scales=h_scales[b][:], in_=hgs[b][:])

        def down(l):
            b, l4 = divmod(l, PB)
            i = UB * b + 2 * PB + l4
            tag = "uo" if l4 % 2 == 0 else "v_ps"
            if b == L // PB - 1 and l4 == 2:
                tag = "wt"
            o_ps = psum.tile([P, 512], F32, name="o_ps", tag=tag, bufs=PS_BUFS[tag])
            for g in range(2):
                cols = slice(256 * l4 + 128 * g, 256 * l4 + 128 * (g + 1))
                nc.tensor.matmul_mx(
                    out=o_ps[:],
                    lhsT=h_codes[b][:, cols].bitcast(FP8X4),
                    lhsT_scale=h_scales[b][:, cols],
                    rhs=codes[i][:, 512 * g : 512 * (g + 1)].bitcast(FP8X4),
                    rhs_scale=scales[i][:, 512 * g : 512 * (g + 1)],
                    start=(g == 0),
                    stop=(g == 1),
                )
            ss = small.tile([P, 1], F32, name="ss", tag="ss")
            junk = junkp.tile([P, 512], BF16, name="junk", tag="junk")
            nc.scalar.activation(out=junk[:], in_=o_ps[:], func=ACT.Square, accum_out=ss[:])
            rno = small.tile([P, 1], F32, name="rno", tag="rno")
            rsqrt_cols(rno[:], ss[:])
            o_sb = ep.tile([P, 512], F32, name="o_sb", tag="o_sb")
            nc.scalar.activation(out=o_sb[:], in_=o_ps[:], func=ACT.Copy, scale=rno[:, 0:1])
            nc.sync.dma_start(out=out[:, l, :], in_=o_sb[:])

        rns[0] = norms(0)

        us = const.tile([P, 8], F32, name="us")
        vs = const.tile([P, 8], F32, name="vs")
        par = const.tile([P, 2], F32, name="par")
        for b in range(2):
            nc.vector.tensor_reduce(out=par[:, b : b + 1], in_=ident[:, b:P:2], op=ALU.add, axis=mybir.AxisListType.X)
        even = const.tile([P, 16], F32, name="even")
        own = const.tile([P, 16], F32, name="own")
        nc.vector.tensor_scalar(out=even[:], in0=gains_raw[:, 0:32:2], scalar1=par[:, 0:1], scalar2=None, op0=ALU.mult)
        nc.vector.scalar_tensor_tensor(
            out=own[:], in0=gains_raw[:, 1:32:2], scalar=par[:, 1:2], in1=even[:], op0=ALU.mult, op1=ALU.add
        )
        nc.scalar.activation(out=vs[:], in_=own[:, 0:8], func=ACT.Abs, scale=math.sqrt(D))
        nc.scalar.activation(out=us[:], in_=own[:, 8:16], func=ACT.Abs)
        xg = const.tile([P, L * D], BF16, name="xg", align_bytes=64)
        x_codes = const.tile([P, L * P], U32, name="x_codes", align_bytes=64)
        x_scales = const.tile([P, L * P], U8, name="x_scales", align_bytes=64)

        def turn_x():
            xw = x_sb[:].bitcast(F32)
            xgw = xg[:].bitcast(F32)
            for lp in range(L // 2):
                xt = psum.tile([P, 4, P], F32, name="xt", tag="wt", bufs=PS_BUFS["wt"])
                for l2 in range(2):
                    for u in range(2):
                        l = 2 * lp + l2
                        nc.tensor.transpose(xt[:, 2 * l2 + u, :], xw[:, 256 * l + u : 256 * (l + 1) : 2], ident[:])
                nc.scalar.copy(
                    out=xgw[:, 512 * lp : 512 * (lp + 1)].rearrange("p (a n u) -> p a n u", a=2, u=2),
                    in_=xt[:].rearrange("p (a u) n -> p a n u", a=2),
                )

        for i in range(1, LEAD):
            rns[i] = norms(i)

        with tc.manual_schedule(engines={mybir.EngineType.DVE}):
            for i in range(NU):
                b, k = divmod(i, UB)
                if i == X_COPY_AT:
                    turn_x()
                prefetch(i)
                scale(i, 0)
                if i == NU - 1:
                    quantise_h(b)
                    down(PB * b)
                    down(PB * b + 1)
                if i > 0:
                    quantise(i - 1)
                if i == X_QUANT_AT:
                    nc.vector.quantize_mx(out=x_codes[:].bitcast(FP8X4), scales=x_scales[:], in_=xg[:])
                if k == 0 and b > 0:
                    down(PB * b - 1)
                if k == 2 * PB:
                    v_round(b, 0)
                    u_round(b, 0)
                    v_round(b, 1)
                if k == 2 * PB + 1:
                    products(b, 1)
                    interleave(b, 0)
                    u_round(b, 2)
                    v_round(b, 3)
                if k == 2 * PB + 2:
                    products(b, 3)
                    interleave(b, 1)
                if i == NU - 1:
                    down(PB * b + 2)
                elif k == 2 * PB + 3:
                    quantise_h(b)
                    for l4 in range(PB - 1):
                        down(PB * b + l4)
                if i == NU - 1:
                    quantise(i, 0, 2048)
                scale(i, 1)
                if k == 2 * PB:
                    products(b, 0)
                    u_round(b, 1)
                    v_round(b, 2)
                if k == 2 * PB + 1:
                    products(b, 2)
                    u_round(b, 3)
            quantise(NU - 1, 2048, 4096)
            down(L - 1)
